import numpy as np
import ml_dtypes


def mxq(x, axis, fmt="e4m3"):
    dtype, down = {"e4m3": (ml_dtypes.float8_e4m3fn, 7), "e5m2": (ml_dtypes.float8_e5m2, 14)}[fmt]
    v = np.moveaxis(np.asarray(x, np.float32).astype(ml_dtypes.bfloat16).astype(np.float64), axis, -1)
    blocks = v.reshape(v.shape[:-1] + (-1, 32))
    amax = np.abs(blocks).max(-1, keepdims=True)
    byte = np.maximum(np.where(amax > 0, np.frexp(amax)[1] - 1 + 127, 0) - down, 1)
    scale = np.exp2(byte - 127.0)
    codes = (blocks / scale).astype(np.float32).astype(dtype).astype(np.float64)
    return np.moveaxis((codes * scale).reshape(v.shape), -1, axis)


WIDE = False


def mx_kscale(k):
    if not WIDE:
        return np.ones(k)
    levels = np.array([10, -10, 5, -5, 0])
    if k % 512:
        return np.exp2(np.random.permutation(np.resize(levels, k // 32))).repeat(32)
    a = np.empty((k // 512, 16))
    for p in range(k // 512):
        a[p, :8] = np.random.permutation(np.resize(levels, 8))
        for g in range(8):
            far = levels[np.abs(levels - a[p, g]) >= 10]
            a[p, g + 8] = far[np.random.randint(len(far))]
    return np.exp2(a.ravel()).repeat(32)


BF16 = ml_dtypes.bfloat16


def bf(x):
    return np.asarray(x, np.float32).astype(BF16)


def f64(x):
    return np.asarray(x).astype(np.float64)


N, F, K, D, E = 256, 16384, 1536, 1024, 512
QS = 2.0
PS = 16.0


def setup_inputs():
    s, t = mx_kscale(F), mx_kscale(E)
    return {"x": bf(np.random.standard_normal((N, F)) * s),
            "Wy_w": bf(np.random.standard_normal((E, F)) * QS * F ** -0.5 / s[None, :] * t[:, None]),
            "Wy_b": bf(np.random.standard_normal(E) * 0.2 * t),
            "k": bf(np.random.standard_normal((K, E)) / t[None, :]),
            "prior": bf(np.random.uniform(size=K) * PS)}


def reference(x, Wy_w, Wy_b, k, prior):
    scale = 1.0 / (E ** 0.5)
    q = (mxq(f64(x), 1, "e4m3") @ mxq(f64(Wy_w), 1, "e4m3").T) + f64(Wy_b)
    sc = (mxq(q, 1, "e4m3") @ mxq(f64(k), 1, "e4m3").T) * scale
    e = np.exp(sc - sc.max(-1, keepdims=True))
    att = e / e.sum(-1, keepdims=True)
    return att * f64(prior)[None, :]

@@ -1,0 +1,272 @@
+from contextlib import ExitStack
+
+import concourse.mybir as mybir
+from concourse.masks import make_identity
+
+F32 = mybir.dt.float32
+BF16 = mybir.dt.bfloat16
+U32 = mybir.dt.uint32
+U8 = mybir.dt.uint8
+FP8X4 = mybir.dt.float8_e4m3fn_x4
+ACT = mybir.ActivationFunctionType
+ALU = mybir.AluOpType
+AXIS = mybir.AxisListType
+
+P = 128
+PASS = 4 * P
+PAIR = 2 * P
+BANK = 512
+
+ROWS, FEATURES, WIDTH, KEYS = 256, 16384, 512, 1536
+PASSES = FEATURES // PASS
+Q_TILES = WIDTH // P
+SCALE = WIDTH ** -0.5
+
+SLOT = 4 * PASS
+SLOTS = FEATURES // SLOT
+SLOT_PASSES = SLOT // PASS
+RAW_BUFS = 4
+LAG = 2
+STAGE_BUFS = 2 * SLOT_PASSES
+PACKED_BUFS = 2 * SLOT_PASSES
+RING = 6
+KEY_PARTS = KEYS // BANK
+
+X_WORDS = PAIR
+W_WORDS = 2 * PAIR
+
+FLOPS = 2 * ROWS * FEATURES * WIDTH + 2 * ROWS * WIDTH * KEYS
+
+
+def piece_widths(slot):
+    if slot == 0:
+        return (PASS, PASS, 2 * PASS)
+    if slot == SLOTS - 1:
+        return (2 * PASS, PASS, PASS)
+    return (SLOT,)
+
+
+def tile_visualdeconfounder_pa_k_kernel(tc, x, Wy_w, Wy_b, k, prior, out):
+    nc = tc.nc
+    w_rows = Wy_w.rearrange("(p t) f -> p t f", t=4)
+    row_blocks = (x.rearrange("(p i) f -> p i f", i=2), w_rows[:, 0:2, :], w_rows[:, 2:4, :])
+
+    with ExitStack() as ctx:
+        ctx.enter_context(tc.manual_schedule())
+        const = ctx.enter_context(tc.tile_pool(name="const", bufs=1))
+        raw_pool = ctx.enter_context(tc.tile_pool(name="raw", bufs=RAW_BUFS))
+        stage = ctx.enter_context(tc.tile_pool(name="stage", bufs=STAGE_BUFS))
+        packed_pool = ctx.enter_context(tc.tile_pool(name="packed", bufs=PACKED_BUFS))
+        small = ctx.enter_context(tc.tile_pool(name="small", bufs=2))
+
+        def load_slot(slot):
+            raw = raw_pool.tile([P, 2 * len(row_blocks), SLOT], BF16)
+            start = 0
+            for width in piece_widths(slot):
+                for b, rows in enumerate(row_blocks):
+                    nc.sync.dma_start(
+                        out=raw[:, 2 * b : 2 * b + 2, start : start + width],
+                        in_=rows[:, :, slot * SLOT + start : slot * SLOT + start + width],
+                    )
+                start += width
+            return raw
+
+        def load_the_rest():
+            nc.sync.dma_start(out=bias_bf16[:], in_=Wy_b.rearrange("(p t) -> p t", t=Q_TILES))
+            nc.gpsimd.tensor_copy(out=bias[:], in_=bias_bf16[:])
+            for part in range(KEY_PARTS):
+                nc.sync.dma_start(
+                    out=keys_raw[:, 4 * part : 4 * part + 4, :],
+                    in_=k[BANK * part : BANK * (part + 1), :].rearrange("(j p) e -> p j e", p=P),
+                )
+            nc.sync.dma_start(out=prior_all[:], in_=prior.partition_broadcast(P))
+
+        ident = const.tile([P, P], F32)
+        make_identity(nc, ident[:])
+        bias_bf16 = const.tile([P, Q_TILES], BF16)
+        bias = const.tile([P, Q_TILES], F32)
+        warm = const.tile([P, 1], F32)
+        nc.vector.memset(warm[:], 0.0)
+        nc.scalar.activation(out=warm[:], in_=warm[:], func=ACT.Exp)
+
+        raws = {}
+        keys_raw = const.tile([P, KEYS // P, WIDTH], BF16)
+        for slot in range(RAW_BUFS):
+            raws[slot] = load_slot(slot)
+
+        key_codes = const.tile([P, KEYS], U32, align_bytes=64)
+        key_scales = const.tile([P, KEYS], U8, align_bytes=64)
+        q_codes = const.tile([P, ROWS], U32, align_bytes=64)
+        q_scales = const.tile([P, ROWS], U8, align_bytes=64)
+        prior_all = const.tile([P, KEYS], BF16)
+
+        with tc.psum_pool(name="acc", bufs=1) as acc_pool, tc.psum_pool(name="ring", bufs=RING) as ring:
+            acc = [acc_pool.tile([P, 2, ROWS], F32, name="acc%d" % u) for u in range(Q_TILES // 2)]
+
+            def transpose_pair(tiles, first, col):
+                bank = ring.tile([P, 2, PAIR], F32)
+                for i in range(2):
+                    words = tiles[:, first + i, col : col + PASS].bitcast(F32)
+                    for u in range(2):
+                        nc.tensor.transpose(bank[:, u, i * P : (i + 1) * P], words[:, u : 2 * P : 2], ident[:])
+                return bank
+
+            def regroup(copy, grouped, first_word, bank):
+                halves = grouped[:].bitcast(F32)[:, 2 * first_word : 2 * (first_word + PAIR)]
+                copy(out=halves.rearrange("p (c u) -> p c u", u=2), in_=bank[:].rearrange("p u c -> p c u"))
+
+            def quantise(grouped, codes, scales, first_word, words):
+                nc.vector.quantize_mx(
+                    out=codes[:, first_word : first_word + words].bitcast(FP8X4),
+                    scales=scales[:, first_word : first_word + words],
+                    in_=grouped[:, 4 * first_word : 4 * (first_word + words)],
+                )
+
+            staged = {}
+            packed = {}
+            key_staged = {}
+
+            def stage_in(run):
+                for g in run:
+                    staged[g] = stage.tile([P, 4 * (X_WORDS + W_WORDS)], BF16, align_bytes=64, name="grouped")
+                for b in range(len(row_blocks)):
+                    for g in run:
+                        bank = transpose_pair(raws[g // SLOT_PASSES], 2 * b, (g % SLOT_PASSES) * PASS)
+                        regroup(nc.vector.tensor_copy if b == 0 else nc.scalar.copy, staged[g], b * PAIR, bank)
+
+            def quantise_run(run):
+                for g in run:
+                    codes = packed_pool.tile([P, X_WORDS + W_WORDS], U32, align_bytes=64)
+                    scales = packed_pool.tile([P, X_WORDS + W_WORDS], U8, align_bytes=64)
+                    packed[g] = (codes, scales)
+                for first_word, words in ((0, X_WORDS), (X_WORDS, W_WORDS)):
+                    for g in run:
+                        quantise(staged[g], packed[g][0], packed[g][1], first_word, words)
+
+            def multiply_pass(g):
+                codes, scales = packed[g]
+                for t in range(Q_TILES):
+                    w_cols = slice(X_WORDS + t * P, X_WORDS + (t + 1) * P)
+                    nc.tensor.matmul_mx(
+                        out=acc[t // 2][:, t % 2, :],
+                        lhsT=codes[:, w_cols].bitcast(FP8X4),
+                        lhsT_scale=scales[:, w_cols],
+                        rhs=codes[:, 0:X_WORDS].bitcast(FP8X4),
+                        rhs_scale=scales[:, 0:X_WORDS],
+                        start=(g == 0 and t % 2 == 0),
+                        stop=(g == PASSES - 1 and t % 2 == 1),
+                    )
+
+            def stage_in_keys(part):
+                grouped = stage.tile([P, 4 * BANK], BF16, align_bytes=64, name="grouped")
+                for half in range(2):
+                    bank = transpose_pair(keys_raw, 4 * part + 2 * half, 0)
+                    regroup(nc.scalar.copy, grouped, half * PAIR, bank)
+                key_staged[part] = grouped
+
+            def quantise_keys(part):
+                nc.vector.quantize_mx(
+                    out=key_codes[:, part * BANK : (part + 1) * BANK].bitcast(FP8X4),
+                    scales=key_scales[:, part * BANK : (part + 1) * BANK],
+                    in_=key_staged[part][:],
+                )
+
+            first = 0
+            for slot in range(SLOTS):
+                for width in piece_widths(slot):
+                    run = range(first, first + width // PASS)
+                    stage_in(run)
+                    quantise_run(run)
+                    for g in run:
+                        if g >= LAG:
+                            multiply_pass(g - LAG)
+                    first += width // PASS
+                if slot + RAW_BUFS < SLOTS:
+                    raws[slot + RAW_BUFS] = load_slot(slot + RAW_BUFS)
+                    if slot + RAW_BUFS == SLOTS - 1:
+                        load_the_rest()
+
+            stage_in_keys(0)
+            stage_in_keys(1)
+            for g in range(PASSES - LAG, PASSES):
+                multiply_pass(g)
+            quantise_keys(0)
+
+            q_planes = const.tile([P, Q_TILES, ROWS], BF16)
+            for t in range(Q_TILES):
+                if t // 2 == 0:
+                    nc.scalar.activation(
+                        out=q_planes[:, t, :], in_=acc[t // 2][:, t % 2, :], func=ACT.Identity, bias=bias[:, t : t + 1]
+                    )
+                else:
+                    nc.vector.tensor_scalar(
+                        out=q_planes[:, t, :],
+                        in0=acc[t // 2][:, t % 2, :],
+                        scalar1=bias[:, t : t + 1],
+                        scalar2=None,
+                        op0=ALU.add,
+                    )
+            stage_in_keys(2)
+            q_grouped = const.tile([P, ROWS, Q_TILES], BF16, align_bytes=64)
+            nc.vector.tensor_copy(out=q_grouped[:], in_=q_planes[:].rearrange("p t c -> p c t"))
+            nc.vector.quantize_mx(
+                out=q_codes[:].bitcast(FP8X4), scales=q_scales[:], in_=q_grouped[:].rearrange("p c t -> p (c t)")
+            )
+            for part in range(1, KEY_PARTS):
+                quantise_keys(part)
+
+        out_rows = out.rearrange("(p i) j -> p i j", i=2)
+        weights = const.tile([P, 2, KEYS], F32)
+        with tc.psum_pool(name="scores", bufs=2 * KEY_PARTS) as score_pool:
+            scores = {}
+            for part in range(KEY_PARTS):
+                for i in range(2):
+                    score = score_pool.tile([P, BANK], F32)
+                    nc.tensor.matmul_mx(
+                        out=score[:],
+                        lhsT=q_codes[:, i * P : (i + 1) * P].bitcast(FP8X4),
+                        lhsT_scale=q_scales[:, i * P : (i + 1) * P],
+                        rhs=key_codes[:, part * BANK : (part + 1) * BANK].bitcast(FP8X4),
+                        rhs_scale=key_scales[:, part * BANK : (part + 1) * BANK],
+                        start=True,
+                        stop=True,
+                    )
+                    scores[i, part] = score
+
+            sums = {}
+            for i in range(2):
+                part_max = small.tile([P, KEY_PARTS], F32)
+                for part in range(KEY_PARTS):
+                    nc.vector.tensor_reduce(out=part_max[:, part : part + 1], in_=scores[i, part][:], axis=AXIS.X, op=ALU.max)
+                row_max = small.tile([P, 1], F32)
+                nc.vector.tensor_reduce(out=row_max[:], in_=part_max[:], axis=AXIS.X, op=ALU.max)
+                shift = small.tile([P, 1], F32)
+                nc.vector.tensor_scalar(out=shift[:], in0=row_max[:], scalar1=-SCALE, scalar2=None, op0=ALU.mult)
+                part_sum = small.tile([P, KEY_PARTS], F32)
+                for part in range(KEY_PARTS):
+                    nc.scalar.activation(
+                        out=weights[:, i, part * BANK : (part + 1) * BANK],
+                        in_=scores[i, part][:],
+                        func=ACT.Exp,
+                        bias=shift[:],
+                        scale=SCALE,
+                        accum_out=part_sum[:, part : part + 1],
+                    )
+                sums[i] = part_sum
+
+            for i in range(2):
+                row_sum = small.tile([P, 1], F32)
+                nc.vector.tensor_reduce(out=row_sum[:], in_=sums[i][:], axis=AXIS.X, op=ALU.add)
+                inverse = small.tile([P, 1], F32)
+                nc.vector.reciprocal(out=inverse[:], in_=row_sum[:])
+                for part in range(KEY_PARTS):
+                    cols = slice(part * BANK, (part + 1) * BANK)
+                    nc.vector.scalar_tensor_tensor(
+                        out=weights[:, i, cols],
+                        in0=weights[:, i, cols],
+                        scalar=inverse[:],
+                        in1=prior_all[:, cols],
+                        op0=ALU.mult,
+                        op1=ALU.mult,
+                    )
+                    nc.sync.dma_start(out=out_rows[:, i, cols], in_=weights[:, i, cols])

@@ -26,9 +26,8 @@ SLOT = 4 * PASS
 SLOTS = FEATURES // SLOT
 SLOT_PASSES = SLOT // PASS
 RAW_BUFS = 4
-LAG = 2
-STAGE_BUFS = 2 * SLOT_PASSES
-PACKED_BUFS = 2 * SLOT_PASSES
+STAGE_BUFS = 4
+PACKED_BUFS = 4
 RING = 6
 KEY_PARTS = KEYS // BANK
 
@@ -55,6 +54,7 @@ def tile_visualdeconfounder_pa_k_kernel(tc, x, Wy_w, Wy_b, k, prior, out):
         ctx.enter_context(tc.manual_schedule())
         const = ctx.enter_context(tc.tile_pool(name="const", bufs=1))
         raw_pool = ctx.enter_context(tc.tile_pool(name="raw", bufs=RAW_BUFS))
+        perm_pool = ctx.enter_context(tc.tile_pool(name="perm", bufs=3))
         stage = ctx.enter_context(tc.tile_pool(name="stage", bufs=STAGE_BUFS))
         packed_pool = ctx.enter_context(tc.tile_pool(name="packed", bufs=PACKED_BUFS))
         small = ctx.enter_context(tc.tile_pool(name="small", bufs=2))
@@ -103,13 +103,36 @@ def tile_visualdeconfounder_pa_k_kernel(tc, x, Wy_w, Wy_b, k, prior, out):
         with tc.psum_pool(name="acc", bufs=1) as acc_pool, tc.psum_pool(name="ring", bufs=RING) as ring:
             acc = [acc_pool.tile([P, 2, ROWS], F32, name="acc%d" % u) for u in range(Q_TILES // 2)]
 
-            def transpose_pair(tiles, first, col):
-                bank = ring.tile([P, 2, PAIR], F32)
+            def transpose_keys(first):
+                bank = ring.tile([P, 2, PAIR], F32, name="bank")
                 for i in range(2):
-                    words = tiles[:, first + i, col : col + PASS].bitcast(F32)
+                    words = keys_raw[:, first + i, :].bitcast(F32)
                     for u in range(2):
                         nc.tensor.transpose(bank[:, u, i * P : (i + 1) * P], words[:, u : 2 * P : 2], ident[:])
                 return bank
+
+            def permute(g):
+                ordered = perm_pool.tile([P, 2 * len(row_blocks), 2, P], F32, name="ordered")
+                col = (g % SLOT_PASSES) * PASS
+                words = raws[g // SLOT_PASSES][:].bitcast(F32)[:, :, col // 2 : (col + PASS) // 2]
+                nc.vector.tensor_copy(out=ordered[:], in_=words.rearrange("p i (w u) -> p i u w", u=2))
+                permuted[g] = ordered
+
+            def transpose_pass(g):
+                banks[g] = []
+                for b in range(len(row_blocks)):
+                    bank = ring.tile([P, 2, PAIR], F32, name="bank")
+                    for i in range(2):
+                        for u in range(2):
+                            nc.tensor.transpose(
+                                bank[:, u, i * P : (i + 1) * P], permuted[g][:, 2 * b + i, u, :], ident[:]
+                            )
+                    banks[g].append(bank)
+
+            def copy_out(g):
+                staged[g] = stage.tile([P, 4 * (X_WORDS + W_WORDS)], BF16, align_bytes=64, name="grouped")
+                for b in range(len(row_blocks)):
+                    regroup(nc.scalar.copy, staged[g], b * PAIR, banks[g][b])
 
             def regroup(copy, grouped, first_word, bank):
                 halves = grouped[:].bitcast(F32)[:, 2 * first_word : 2 * (first_word + PAIR)]
@@ -122,26 +145,18 @@ def tile_visualdeconfounder_pa_k_kernel(tc, x, Wy_w, Wy_b, k, prior, out):
                     in_=grouped[:, 4 * first_word : 4 * (first_word + words)],
                 )
 
+            permuted = {}
+            banks = {}
             staged = {}
             packed = {}
             key_staged = {}
 
-            def stage_in(run):
-                for g in run:
-                    staged[g] = stage.tile([P, 4 * (X_WORDS + W_WORDS)], BF16, align_bytes=64, name="grouped")
-                for b in range(len(row_blocks)):
-                    for g in run:
-                        bank = transpose_pair(raws[g // SLOT_PASSES], 2 * b, (g % SLOT_PASSES) * PASS)
-                        regroup(nc.vector.tensor_copy if b == 0 else nc.scalar.copy, staged[g], b * PAIR, bank)
-
-            def quantise_run(run):
-                for g in run:
-                    codes = packed_pool.tile([P, X_WORDS + W_WORDS], U32, align_bytes=64)
-                    scales = packed_pool.tile([P, X_WORDS + W_WORDS], U8, align_bytes=64)
-                    packed[g] = (codes, scales)
+            def quantise_pass(g):
+                codes = packed_pool.tile([P, X_WORDS + W_WORDS], U32, align_bytes=64, name="codes")
+                scales = packed_pool.tile([P, X_WORDS + W_WORDS], U8, align_bytes=64, name="scales")
+                packed[g] = (codes, scales)
                 for first_word, words in ((0, X_WORDS), (X_WORDS, W_WORDS)):
-                    for g in run:
-                        quantise(staged[g], packed[g][0], packed[g][1], first_word, words)
+                    quantise(staged[g], codes, scales, first_word, words)
 
             def multiply_pass(g):
                 codes, scales = packed[g]
@@ -160,7 +175,7 @@ def tile_visualdeconfounder_pa_k_kernel(tc, x, Wy_w, Wy_b, k, prior, out):
             def stage_in_keys(part):
                 grouped = stage.tile([P, 4 * BANK], BF16, align_bytes=64, name="grouped")
                 for half in range(2):
-                    bank = transpose_pair(keys_raw, 4 * part + 2 * half, 0)
+                    bank = transpose_keys(4 * part + 2 * half)
                     regroup(nc.scalar.copy, grouped, half * PAIR, bank)
                 key_staged[part] = grouped
 
@@ -171,24 +186,24 @@ def tile_visualdeconfounder_pa_k_kernel(tc, x, Wy_w, Wy_b, k, prior, out):
                     in_=key_staged[part][:],
                 )
 
-            first = 0
-            for slot in range(SLOTS):
-                for width in piece_widths(slot):
-                    run = range(first, first + width // PASS)
-                    stage_in(run)
-                    quantise_run(run)
-                    for g in run:
-                        if g >= LAG:
-                            multiply_pass(g - LAG)
-                    first += width // PASS
-                if slot + RAW_BUFS < SLOTS:
+            for s in range(PASSES):
+                permute(s)
+                if s >= 3:
+                    multiply_pass(s - 3)
+                transpose_pass(s)
+                copy_out(s)
+                if s >= 2:
+                    quantise_pass(s - 2)
+                slot = s // SLOT_PASSES
+                if s % SLOT_PASSES == SLOT_PASSES - 1 and slot + RAW_BUFS < SLOTS:
                     raws[slot + RAW_BUFS] = load_slot(slot + RAW_BUFS)
                     if slot + RAW_BUFS == SLOTS - 1:
                         load_the_rest()
 
-            stage_in_keys(0)
-            stage_in_keys(1)
-            for g in range(PASSES - LAG, PASSES):
+            multiply_pass(PASSES - 3)
+            for g in (PASSES - 2, PASSES - 1):
+                stage_in_keys(g - (PASSES - 2))
+                quantise_pass(g)
                 multiply_pass(g)
             quantise_keys(0)
 

@@ -22,10 +22,8 @@ PASSES = FEATURES // PASS
 Q_TILES = WIDTH // P
 SCALE = WIDTH ** -0.5
 
-SLOT = 4 * PASS
-SLOTS = FEATURES // SLOT
-SLOT_PASSES = SLOT // PASS
-RAW_BUFS = 4
+CHUNKS = (1, 1) + 14 * (2,) + (1, 1)
+RAW_BUFS = {1: 2, 2: 6}
 STAGE_BUFS = 4
 PACKED_BUFS = 4
 RING = 6
@@ -37,14 +35,6 @@ W_WORDS = 2 * PAIR
 FLOPS = 2 * ROWS * FEATURES * WIDTH + 2 * ROWS * WIDTH * KEYS
 
 
-def piece_widths(slot):
-    if slot == 0:
-        return (PASS, PASS, 2 * PASS)
-    if slot == SLOTS - 1:
-        return (2 * PASS, PASS, PASS)
-    return (SLOT,)
-
-
 def tile_visualdeconfounder_pa_k_kernel(tc, x, Wy_w, Wy_b, k, prior, out):
     nc = tc.nc
     w_rows = Wy_w.rearrange("(p t) f -> p t f", t=4)
@@ -53,23 +43,22 @@ def tile_visualdeconfounder_pa_k_kernel(tc, x, Wy_w, Wy_b, k, prior, out):
     with ExitStack() as ctx:
         ctx.enter_context(tc.manual_schedule())
         const = ctx.enter_context(tc.tile_pool(name="const", bufs=1))
-        raw_pool = ctx.enter_context(tc.tile_pool(name="raw", bufs=RAW_BUFS))
-        perm_pool = ctx.enter_context(tc.tile_pool(name="perm", bufs=3))
+        raw_pool = ctx.enter_context(tc.tile_pool(name="raw", bufs=1))
+        perm_pool = ctx.enter_context(tc.tile_pool(name="perm", bufs=4))
         stage = ctx.enter_context(tc.tile_pool(name="stage", bufs=STAGE_BUFS))
         packed_pool = ctx.enter_context(tc.tile_pool(name="packed", bufs=PACKED_BUFS))
         small = ctx.enter_context(tc.tile_pool(name="small", bufs=2))
 
-        def load_slot(slot):
-            raw = raw_pool.tile([P, 2 * len(row_blocks), SLOT], BF16)
-            start = 0
-            for width in piece_widths(slot):
-                for b, rows in enumerate(row_blocks):
-                    nc.sync.dma_start(
-                        out=raw[:, 2 * b : 2 * b + 2, start : start + width],
-                        in_=rows[:, :, slot * SLOT + start : slot * SLOT + start + width],
-                    )
-                start += width
-            return raw
+        def load_chunk(first, passes):
+            raw = raw_pool.tile(
+                [P, 2 * len(row_blocks), passes * PASS], BF16, bufs=RAW_BUFS[passes], name="raw%d" % passes
+            )
+            for b, rows in enumerate(row_blocks):
+                nc.sync.dma_start(
+                    out=raw[:, 2 * b : 2 * b + 2, :], in_=rows[:, :, first * PASS : (first + passes) * PASS]
+                )
+            for g in range(passes):
+                raws[first + g] = raw[:, :, g * PASS : (g + 1) * PASS]
 
         def load_the_rest():
             nc.sync.dma_start(out=bias_bf16[:], in_=Wy_b.rearrange("(p t) -> p t", t=Q_TILES))
@@ -91,14 +80,16 @@ def tile_visualdeconfounder_pa_k_kernel(tc, x, Wy_w, Wy_b, k, prior, out):
 
         raws = {}
         keys_raw = const.tile([P, KEYS // P, WIDTH], BF16)
-        for slot in range(RAW_BUFS):
-            raws[slot] = load_slot(slot)
+        prior_all = const.tile([P, KEYS], BF16)
+        chunks = [(sum(CHUNKS[:c]), passes) for c, passes in enumerate(CHUNKS)]
+        for first, passes in chunks:
+            load_chunk(first, passes)
+        load_the_rest()
 
         key_codes = const.tile([P, KEYS], U32, align_bytes=64)
         key_scales = const.tile([P, KEYS], U8, align_bytes=64)
         q_codes = const.tile([P, ROWS], U32, align_bytes=64)
         q_scales = const.tile([P, ROWS], U8, align_bytes=64)
-        prior_all = const.tile([P, KEYS], BF16)
 
         with tc.psum_pool(name="acc", bufs=1) as acc_pool, tc.psum_pool(name="ring", bufs=RING) as ring:
             acc = [acc_pool.tile([P, 2, ROWS], F32, name="acc%d" % u) for u in range(Q_TILES // 2)]
@@ -113,9 +104,7 @@ def tile_visualdeconfounder_pa_k_kernel(tc, x, Wy_w, Wy_b, k, prior, out):
 
             def permute(g):
                 ordered = perm_pool.tile([P, 2 * len(row_blocks), 2, P], F32, name="ordered")
-                col = (g % SLOT_PASSES) * PASS
-                words = raws[g // SLOT_PASSES][:].bitcast(F32)[:, :, col // 2 : (col + PASS) // 2]
-                nc.vector.tensor_copy(out=ordered[:], in_=words.rearrange("p i (w u) -> p i u w", u=2))
+                nc.vector.tensor_copy(out=ordered[:], in_=raws[g].bitcast(F32).rearrange("p i (w u) -> p i u w", u=2))
                 permuted[g] = ordered
 
             def transpose_pass(g):
@@ -151,12 +140,14 @@ def tile_visualdeconfounder_pa_k_kernel(tc, x, Wy_w, Wy_b, k, prior, out):
             packed = {}
             key_staged = {}
 
-            def quantise_pass(g):
-                codes = packed_pool.tile([P, X_WORDS + W_WORDS], U32, align_bytes=64, name="codes")
-                scales = packed_pool.tile([P, X_WORDS + W_WORDS], U8, align_bytes=64, name="scales")
-                packed[g] = (codes, scales)
-                for first_word, words in ((0, X_WORDS), (X_WORDS, W_WORDS)):
-                    quantise(staged[g], codes, scales, first_word, words)
+            def quantise_run(run):
+                for g in run:
+                    codes = packed_pool.tile([P, X_WORDS + W_WORDS], U32, align_bytes=64, name="codes")
+                    scales = packed_pool.tile([P, X_WORDS + W_WORDS], U8, align_bytes=64, name="scales")
+                    packed[g] = (codes, scales)
+                for g in run:
+                    for first_word, words in ((0, X_WORDS), (X_WORDS, W_WORDS)):
+                        quantise(staged[g], packed[g][0], packed[g][1], first_word, words)
 
             def multiply_pass(g):
                 codes, scales = packed[g]
@@ -186,25 +177,25 @@ def tile_visualdeconfounder_pa_k_kernel(tc, x, Wy_w, Wy_b, k, prior, out):
                     in_=key_staged[part][:],
                 )
 
-            for s in range(PASSES):
-                permute(s)
-                if s >= 3:
-                    multiply_pass(s - 3)
-                transpose_pass(s)
-                copy_out(s)
-                if s >= 2:
-                    quantise_pass(s - 2)
-                slot = s // SLOT_PASSES
-                if s % SLOT_PASSES == SLOT_PASSES - 1 and slot + RAW_BUFS < SLOTS:
-                    raws[slot + RAW_BUFS] = load_slot(slot + RAW_BUFS)
-                    if slot + RAW_BUFS == SLOTS - 1:
-                        load_the_rest()
+            runs = [range(first, first + passes) for first, passes in chunks]
+            for n, run in enumerate(runs):
+                for g in run:
+                    permute(g)
+                if n >= 2:
+                    for g in runs[n - 2]:
+                        multiply_pass(g)
+                for g in run:
+                    transpose_pass(g)
+                for g in run:
+                    copy_out(g)
+                if n >= 1:
+                    quantise_run(runs[n - 1])
 
-            multiply_pass(PASSES - 3)
-            for g in (PASSES - 2, PASSES - 1):
-                stage_in_keys(g - (PASSES - 2))
-                quantise_pass(g)
-                multiply_pass(g)
+            multiply_pass(PASSES - 2)
+            stage_in_keys(0)
+            quantise_run(runs[-1])
+            stage_in_keys(1)
+            multiply_pass(PASSES - 1)
             quantise_keys(0)
 
             q_planes = const.tile([P, Q_TILES, ROWS], BF16)

@@ -140,14 +140,12 @@ def tile_visualdeconfounder_pa_k_kernel(tc, x, Wy_w, Wy_b, k, prior, out):
             packed = {}
             key_staged = {}
 
-            def quantise_run(run):
-                for g in run:
-                    codes = packed_pool.tile([P, X_WORDS + W_WORDS], U32, align_bytes=64, name="codes")
-                    scales = packed_pool.tile([P, X_WORDS + W_WORDS], U8, align_bytes=64, name="scales")
-                    packed[g] = (codes, scales)
-                for g in run:
-                    for first_word, words in ((0, X_WORDS), (X_WORDS, W_WORDS)):
-                        quantise(staged[g], packed[g][0], packed[g][1], first_word, words)
+            def quantise_pass(g):
+                codes = packed_pool.tile([P, X_WORDS + W_WORDS], U32, align_bytes=64, name="codes")
+                scales = packed_pool.tile([P, X_WORDS + W_WORDS], U8, align_bytes=64, name="scales")
+                packed[g] = (codes, scales)
+                for first_word, words in ((0, X_WORDS), (X_WORDS, W_WORDS)):
+                    quantise(staged[g], codes, scales, first_word, words)
 
             def multiply_pass(g):
                 codes, scales = packed[g]
@@ -177,25 +175,20 @@ def tile_visualdeconfounder_pa_k_kernel(tc, x, Wy_w, Wy_b, k, prior, out):
                     in_=key_staged[part][:],
                 )
 
-            runs = [range(first, first + passes) for first, passes in chunks]
-            for n, run in enumerate(runs):
-                for g in run:
-                    permute(g)
-                if n >= 2:
-                    for g in runs[n - 2]:
-                        multiply_pass(g)
-                for g in run:
-                    transpose_pass(g)
-                for g in run:
-                    copy_out(g)
-                if n >= 1:
-                    quantise_run(runs[n - 1])
+            for s in range(PASSES):
+                permute(s)
+                if s >= 3:
+                    multiply_pass(s - 3)
+                transpose_pass(s)
+                copy_out(s)
+                if s >= 2:
+                    quantise_pass(s - 2)
 
-            multiply_pass(PASSES - 2)
-            stage_in_keys(0)
-            quantise_run(runs[-1])
-            stage_in_keys(1)
-            multiply_pass(PASSES - 1)
+            multiply_pass(PASSES - 3)
+            for g in (PASSES - 2, PASSES - 1):
+                stage_in_keys(g - (PASSES - 2))
+                quantise_pass(g)
+                multiply_pass(g)
             quantise_keys(0)
 
             q_planes = const.tile([P, Q_TILES, ROWS], BF16)

@@ -103,9 +103,17 @@ def tile_visualdeconfounder_pa_k_kernel(tc, x, Wy_w, Wy_b, k, prior, out):
                 return bank
 
             def permute(g):
-                ordered = perm_pool.tile([P, 2 * len(row_blocks), 2, P], F32, name="ordered")
-                nc.vector.tensor_copy(out=ordered[:], in_=raws[g].bitcast(F32).rearrange("p i (w u) -> p i u w", u=2))
-                permuted[g] = ordered
+                seconds = perm_pool.tile([P, 2 * len(row_blocks), P], F32, name="seconds")
+                words = raws[g].bitcast(F32)
+                nc.vector.tensor_copy(
+                    out=seconds[:].rearrange("p i (c h j) -> p i c h j", h=2, j=8),
+                    in_=words.rearrange("p i (h c u j) -> p i u c h j", h=2, u=2, j=8)[:, :, 1],
+                )
+                permuted[g] = (words[:, :, 0:P], seconds[:])
+
+            def permute_in_place(g):
+                windows = raws[g].bitcast(F32).rearrange("p i (h c u j) -> p i h c u j", h=2, u=2, j=8)
+                nc.vector.tensor_copy(out=windows[:, :, 0, :, 1, :], in_=windows[:, :, 1, :, 0, :])
 
             def transpose_pass(g):
                 banks[g] = []
@@ -114,7 +122,7 @@ def tile_visualdeconfounder_pa_k_kernel(tc, x, Wy_w, Wy_b, k, prior, out):
                     for i in range(2):
                         for u in range(2):
                             nc.tensor.transpose(
-                                bank[:, u, i * P : (i + 1) * P], permuted[g][:, 2 * b + i, u, :], ident[:]
+                                bank[:, u, i * P : (i + 1) * P], permuted[g][u][:, 2 * b + i, :], ident[:]
                             )
                     banks[g].append(bank)
 
@@ -140,12 +148,17 @@ def tile_visualdeconfounder_pa_k_kernel(tc, x, Wy_w, Wy_b, k, prior, out):
             packed = {}
             key_staged = {}
 
-            def quantise_pass(g):
+            def pack(g):
                 codes = packed_pool.tile([P, X_WORDS + W_WORDS], U32, align_bytes=64, name="codes")
                 scales = packed_pool.tile([P, X_WORDS + W_WORDS], U8, align_bytes=64, name="scales")
                 packed[g] = (codes, scales)
-                for first_word, words in ((0, X_WORDS), (X_WORDS, W_WORDS)):
-                    quantise(staged[g], codes, scales, first_word, words)
+
+            def quantise_x(g):
+                pack(g)
+                quantise(staged[g], packed[g][0], packed[g][1], 0, X_WORDS)
+
+            def quantise_w(g):
+                quantise(staged[g], packed[g][0], packed[g][1], X_WORDS, W_WORDS)
 
             def multiply_pass(g):
                 codes, scales = packed[g]
@@ -175,19 +188,27 @@ def tile_visualdeconfounder_pa_k_kernel(tc, x, Wy_w, Wy_b, k, prior, out):
                     in_=key_staged[part][:],
                 )
 
+            permute(0)
+            permute_in_place(0)
             for s in range(PASSES):
-                permute(s)
+                if s + 1 < PASSES:
+                    permute(s + 1)
+                if s >= 2:
+                    quantise_x(s - 2)
+                if s + 1 < PASSES:
+                    permute_in_place(s + 1)
+                if s >= 2:
+                    quantise_w(s - 2)
                 if s >= 3:
                     multiply_pass(s - 3)
                 transpose_pass(s)
                 copy_out(s)
-                if s >= 2:
-                    quantise_pass(s - 2)
 
             multiply_pass(PASSES - 3)
             for g in (PASSES - 2, PASSES - 1):
                 stage_in_keys(g - (PASSES - 2))
-                quantise_pass(g)
+                quantise_x(g)
+                quantise_w(g)
                 multiply_pass(g)
             quantise_keys(0)
 

@@ -22,12 +22,15 @@ PASSES = FEATURES // PASS
 Q_TILES = WIDTH // P
 SCALE = WIDTH ** -0.5
 
-CHUNKS = (1, 1) + 14 * (2,) + (1, 1)
-RAW_BUFS = {1: 2, 2: 6}
-STAGE_BUFS = 4
-PACKED_BUFS = 4
+CHUNKS = (1, 1, 2) + 6 * (4,) + (2, 1, 1)
+LONG = max(CHUNKS)
+RAW_BUFS = {1: 6, 2: 3, 4: 9}
+PERM_BUFS = 4
+STAGE_BUFS = 10
+PACKED_BUFS = 9
 RING = 6
 KEY_PARTS = KEYS // BANK
+STEP = 3
 
 X_WORDS = PAIR
 W_WORDS = 2 * PAIR
@@ -47,18 +50,15 @@ def tile_visualdeconfounder_pa_k_kernel(tc, x, Wy_w, Wy_b, k, prior, out):
         perm_pool = ctx.enter_context(tc.tile_pool(name="perm", bufs=4))
         stage = ctx.enter_context(tc.tile_pool(name="stage", bufs=STAGE_BUFS))
         packed_pool = ctx.enter_context(tc.tile_pool(name="packed", bufs=PACKED_BUFS))
-        small = ctx.enter_context(tc.tile_pool(name="small", bufs=2))
+        small = ctx.enter_context(tc.tile_pool(name="small", bufs=6))
 
-        def load_chunk(first, passes):
-            raw = raw_pool.tile(
-                [P, 2 * len(row_blocks), passes * PASS], BF16, bufs=RAW_BUFS[passes], name="raw%d" % passes
+        def load_unit(first, passes, b):
+            raw = raw_pool.tile([P, 2 * passes, PASS], BF16, bufs=RAW_BUFS[passes], name="raw%d" % passes)
+            nc.sync.dma_start(
+                out=raw[:].rearrange("p (i g) f -> p i (g f)", i=2),
+                in_=row_blocks[b][:, :, first * PASS : (first + passes) * PASS],
             )
-            for b, rows in enumerate(row_blocks):
-                nc.sync.dma_start(
-                    out=raw[:, 2 * b : 2 * b + 2, :], in_=rows[:, :, first * PASS : (first + passes) * PASS]
-                )
-            for g in range(passes):
-                raws[first + g] = raw[:, :, g * PASS : (g + 1) * PASS]
+            return raw
 
         def load_the_rest():
             nc.sync.dma_start(out=bias_bf16[:], in_=Wy_b.rearrange("(p t) -> p t", t=Q_TILES))
@@ -78,18 +78,19 @@ def tile_visualdeconfounder_pa_k_kernel(tc, x, Wy_w, Wy_b, k, prior, out):
         nc.vector.memset(warm[:], 0.0)
         nc.scalar.activation(out=warm[:], in_=warm[:], func=ACT.Exp)
 
-        raws = {}
         keys_raw = const.tile([P, KEYS // P, WIDTH], BF16)
         prior_all = const.tile([P, KEYS], BF16)
-        chunks = [(sum(CHUNKS[:c]), passes) for c, passes in enumerate(CHUNKS)]
-        for first, passes in chunks:
-            load_chunk(first, passes)
+        raws = []
+        unit_passes = []
+        atoms = []
+        for c, passes in enumerate(CHUNKS):
+            first = sum(CHUNKS[:c])
+            for b in range(len(row_blocks)):
+                atoms.extend((len(raws), b, first + g, g) for g in range(passes))
+                raws.append(load_unit(first, passes, b))
+                unit_passes.append(passes)
         load_the_rest()
 
-        key_codes = const.tile([P, KEYS], U32, align_bytes=64)
-        key_scales = const.tile([P, KEYS], U8, align_bytes=64)
-        q_codes = const.tile([P, ROWS], U32, align_bytes=64)
-        q_scales = const.tile([P, ROWS], U8, align_bytes=64)
 
         with tc.psum_pool(name="acc", bufs=1) as acc_pool, tc.psum_pool(name="ring", bufs=RING) as ring:
             acc = [acc_pool.tile([P, 2, ROWS], F32, name="acc%d" % u) for u in range(Q_TILES // 2)]
@@ -102,63 +103,54 @@ def tile_visualdeconfounder_pa_k_kernel(tc, x, Wy_w, Wy_b, k, prior, out):
                         nc.tensor.transpose(bank[:, u, i * P : (i + 1) * P], words[:, u : 2 * P : 2], ident[:])
                 return bank
 
-            def permute(g):
-                seconds = perm_pool.tile([P, 2 * len(row_blocks), P], F32, name="seconds")
-                words = raws[g].bitcast(F32)
+            def permute(n):
+                seconds = perm_pool.tile([P, 2 * LONG, P], F32, name="seconds")
+                words = raws[n][:].bitcast(F32)
+                rows = 2 * unit_passes[n]
                 nc.vector.tensor_copy(
-                    out=seconds[:].rearrange("p i (c h j) -> p i c h j", h=2, j=8),
-                    in_=words.rearrange("p i (h c u j) -> p i u c h j", h=2, u=2, j=8)[:, :, 1],
+                    out=seconds[:, 0:rows].rearrange("p r (c h j) -> p r c h j", h=2, j=8),
+                    in_=words.rearrange("p r (h c u j) -> p r u c h j", h=2, u=2, j=8)[:, :, 1],
                 )
-                permuted[g] = (words[:, :, 0:P], seconds[:])
+                permuted[n] = (words[:, :, 0:P], seconds[:])
 
-            def permute_in_place(g):
-                windows = raws[g].bitcast(F32).rearrange("p i (h c u j) -> p i h c u j", h=2, u=2, j=8)
+            def permute_in_place(n):
+                windows = raws[n][:].bitcast(F32).rearrange("p r (h c u j) -> p r h c u j", h=2, u=2, j=8)
                 nc.vector.tensor_copy(out=windows[:, :, 0, :, 1, :], in_=windows[:, :, 1, :, 0, :])
 
-            def transpose_pass(g):
-                banks[g] = []
-                for b in range(len(row_blocks)):
-                    bank = ring.tile([P, 2, PAIR], F32, name="bank")
-                    for i in range(2):
-                        for u in range(2):
-                            nc.tensor.transpose(
-                                bank[:, u, i * P : (i + 1) * P], permuted[g][u][:, 2 * b + i, :], ident[:]
-                            )
-                    banks[g].append(bank)
+            def transpose_atom(n, b, p, g):
+                passes = unit_passes[n]
+                bank = ring.tile([P, 2, PAIR], F32, name="bank")
+                for i in range(2):
+                    for u in range(2):
+                        nc.tensor.transpose(
+                            bank[:, u, i * P : (i + 1) * P], permuted[n][u][:, i * passes + g, :], ident[:]
+                        )
+                banks[b, p] = bank
 
-            def copy_out(g):
-                staged[g] = stage.tile([P, 4 * (X_WORDS + W_WORDS)], BF16, align_bytes=64, name="grouped")
-                for b in range(len(row_blocks)):
-                    regroup(nc.scalar.copy, staged[g], b * PAIR, banks[g][b])
+            def copy_out(b, p):
+                staged[b, p] = stage.tile([P, 4 * PAIR], BF16, align_bytes=64, name="grouped")
+                regroup(nc.scalar.copy, staged[b, p], 0, banks[b, p])
 
             def regroup(copy, grouped, first_word, bank):
                 halves = grouped[:].bitcast(F32)[:, 2 * first_word : 2 * (first_word + PAIR)]
                 copy(out=halves.rearrange("p (c u) -> p c u", u=2), in_=bank[:].rearrange("p u c -> p c u"))
-
-            def quantise(grouped, codes, scales, first_word, words):
-                nc.vector.quantize_mx(
-                    out=codes[:, first_word : first_word + words].bitcast(FP8X4),
-                    scales=scales[:, first_word : first_word + words],
-                    in_=grouped[:, 4 * first_word : 4 * (first_word + words)],
-                )
 
             permuted = {}
             banks = {}
             staged = {}
             packed = {}
             key_staged = {}
+            key_packed = {}
 
-            def pack(g):
-                codes = packed_pool.tile([P, X_WORDS + W_WORDS], U32, align_bytes=64, name="codes")
-                scales = packed_pool.tile([P, X_WORDS + W_WORDS], U8, align_bytes=64, name="scales")
-                packed[g] = (codes, scales)
-
-            def quantise_x(g):
-                pack(g)
-                quantise(staged[g], packed[g][0], packed[g][1], 0, X_WORDS)
-
-            def quantise_w(g):
-                quantise(staged[g], packed[g][0], packed[g][1], X_WORDS, W_WORDS)
+            def quantise(b, p):
+                if p not in packed:
+                    codes = packed_pool.tile([P, X_WORDS + W_WORDS], U32, align_bytes=64, name="codes")
+                    scales = packed_pool.tile([P, X_WORDS + W_WORDS], U8, align_bytes=64, name="scales")
+                    packed[p] = (codes, scales)
+                cols = slice(b * PAIR, (b + 1) * PAIR)
+                nc.vector.quantize_mx(
+                    out=packed[p][0][:, cols].bitcast(FP8X4), scales=packed[p][1][:, cols], in_=staged[b, p][:]
+                )
 
             def multiply_pass(g):
                 codes, scales = packed[g]
@@ -175,118 +167,152 @@ def tile_visualdeconfounder_pa_k_kernel(tc, x, Wy_w, Wy_b, k, prior, out):
                     )
 
             def stage_in_keys(part):
-                grouped = stage.tile([P, 4 * BANK], BF16, align_bytes=64, name="grouped")
+                grouped = const.tile([P, 4 * BANK], BF16, align_bytes=64, name="key_grouped%d" % part)
                 for half in range(2):
                     bank = transpose_keys(4 * part + 2 * half)
                     regroup(nc.scalar.copy, grouped, half * PAIR, bank)
                 key_staged[part] = grouped
 
             def quantise_keys(part):
-                nc.vector.quantize_mx(
-                    out=key_codes[:, part * BANK : (part + 1) * BANK].bitcast(FP8X4),
-                    scales=key_scales[:, part * BANK : (part + 1) * BANK],
-                    in_=key_staged[part][:],
-                )
+                codes = const.tile([P, BANK], U32, align_bytes=64, name="key_codes%d" % part)
+                scales = const.tile([P, BANK], U8, align_bytes=64, name="key_scales%d" % part)
+                key_packed[part] = (codes, scales)
+                nc.vector.quantize_mx(out=codes[:].bitcast(FP8X4), scales=scales[:], in_=key_staged[part][:])
 
-            permute(0)
-            permute_in_place(0)
-            for s in range(PASSES):
-                if s + 1 < PASSES:
-                    permute(s + 1)
+            steps = [atoms[a : a + STEP] for a in range(0, len(atoms), STEP)]
+            starts = [[n for n, b, p, g in step if g == 0] for step in steps]
+            for n in starts[0]:
+                permute(n)
+                permute_in_place(n)
+            waiting = list(range(PASSES))
+            quantised = set()
+            for s in range(len(steps) + 2):
+                done = [p for p in waiting if all((b, p) in quantised for b in range(len(row_blocks)))]
+                ahead = starts[s + 1] if s + 1 < len(steps) else []
+                for n in ahead:
+                    permute(n)
                 if s >= 2:
-                    quantise_x(s - 2)
-                if s + 1 < PASSES:
-                    permute_in_place(s + 1)
-                if s >= 2:
-                    quantise_w(s - 2)
-                if s >= 3:
-                    multiply_pass(s - 3)
-                transpose_pass(s)
-                copy_out(s)
-
-            multiply_pass(PASSES - 3)
-            for g in (PASSES - 2, PASSES - 1):
-                stage_in_keys(g - (PASSES - 2))
-                quantise_x(g)
-                quantise_w(g)
-                multiply_pass(g)
+                    for n, b, p, g in steps[s - 2]:
+                        quantise(b, p)
+                        quantised.add((b, p))
+                for n in ahead:
+                    permute_in_place(n)
+                for p in done[: 1 if s < len(steps) else None]:
+                    multiply_pass(p)
+                    waiting.remove(p)
+                if s < len(steps):
+                    for n, b, p, g in steps[s]:
+                        transpose_atom(n, b, p, g)
+                    for n, b, p, g in steps[s]:
+                        copy_out(b, p)
+                if s == len(steps):
+                    stage_in_keys(0)
+            for p in waiting:
+                multiply_pass(p)
             quantise_keys(0)
 
-            q_planes = const.tile([P, Q_TILES, ROWS], BF16)
-            for t in range(Q_TILES):
-                if t // 2 == 0:
-                    nc.scalar.activation(
-                        out=q_planes[:, t, :], in_=acc[t // 2][:, t % 2, :], func=ACT.Identity, bias=bias[:, t : t + 1]
-                    )
-                else:
-                    nc.vector.tensor_scalar(
-                        out=q_planes[:, t, :],
-                        in0=acc[t // 2][:, t % 2, :],
-                        scalar1=bias[:, t : t + 1],
-                        scalar2=None,
-                        op0=ALU.add,
-                    )
-            stage_in_keys(2)
-            q_grouped = const.tile([P, ROWS, Q_TILES], BF16, align_bytes=64)
-            nc.vector.tensor_copy(out=q_grouped[:], in_=q_planes[:].rearrange("p t c -> p c t"))
-            nc.vector.quantize_mx(
-                out=q_codes[:].bitcast(FP8X4), scales=q_scales[:], in_=q_grouped[:].rearrange("p c t -> p (c t)")
-            )
-            for part in range(1, KEY_PARTS):
-                quantise_keys(part)
-
-        out_rows = out.rearrange("(p i) j -> p i j", i=2)
-        weights = const.tile([P, 2, KEYS], F32)
-        with tc.psum_pool(name="scores", bufs=2 * KEY_PARTS) as score_pool:
-            scores = {}
-            for part in range(KEY_PARTS):
-                for i in range(2):
-                    score = score_pool.tile([P, BANK], F32)
-                    nc.tensor.matmul_mx(
-                        out=score[:],
-                        lhsT=q_codes[:, i * P : (i + 1) * P].bitcast(FP8X4),
-                        lhsT_scale=q_scales[:, i * P : (i + 1) * P],
-                        rhs=key_codes[:, part * BANK : (part + 1) * BANK].bitcast(FP8X4),
-                        rhs_scale=key_scales[:, part * BANK : (part + 1) * BANK],
-                        start=True,
-                        stop=True,
-                    )
-                    scores[i, part] = score
-
-            sums = {}
+            q_planes = []
             for i in range(2):
-                part_max = small.tile([P, KEY_PARTS], F32)
+                planes = const.tile([P, Q_TILES, P], BF16, name="q_planes%d" % i)
+                q_planes.append(planes)
+                for t in range(Q_TILES):
+                    source = acc[t // 2][:, t % 2, i * P : (i + 1) * P]
+                    if t // 2 == 0:
+                        nc.scalar.activation(
+                            out=planes[:, t, :], in_=source, func=ACT.Identity, bias=bias[:, t : t + 1]
+                        )
+                    else:
+                        nc.vector.tensor_scalar(
+                            out=planes[:, t, :], in0=source, scalar1=bias[:, t : t + 1], scalar2=None, op0=ALU.add
+                        )
+            stage_in_keys(1)
+            stage_in_keys(2)
+            q_packed = []
+            for i in range(2):
+                grouped = const.tile([P, P, Q_TILES], BF16, align_bytes=64, name="q_grouped%d" % i)
+                nc.vector.tensor_copy(out=grouped[:], in_=q_planes[i][:].rearrange("p t c -> p c t"))
+                codes = const.tile([P, P], U32, align_bytes=64, name="q_codes%d" % i)
+                scales = const.tile([P, P], U8, align_bytes=64, name="q_scales%d" % i)
+                q_packed.append((codes, scales, grouped))
+            for codes, scales, grouped in q_packed:
+                nc.vector.quantize_mx(
+                    out=codes[:].bitcast(FP8X4), scales=scales[:], in_=grouped[:].rearrange("p c t -> p (c t)")
+                )
+
+            scores = {}
+
+            def score(i, part):
+                bank = ring.tile([P, 2, PAIR], F32, name="bank")
+                scores[i, part] = bank[:].rearrange("p u c -> p (u c)")
+                nc.tensor.matmul_mx(
+                    out=scores[i, part],
+                    lhsT=q_packed[i][0][:].bitcast(FP8X4),
+                    lhsT_scale=q_packed[i][1][:],
+                    rhs=key_packed[part][0][:].bitcast(FP8X4),
+                    rhs_scale=key_packed[part][1][:],
+                    start=True,
+                    stop=True,
+                )
+
+            part_max = [small.tile([P, KEY_PARTS], F32, name="part_max%d" % i) for i in range(2)]
+            part_sum = [small.tile([P, KEY_PARTS], F32, name="part_sum%d" % i) for i in range(2)]
+            weights = {}
+
+            def maximum(i, part):
+                nc.vector.tensor_reduce(
+                    out=part_max[i][:, part : part + 1], in_=scores[i, part], axis=AXIS.X, op=ALU.max
+                )
+
+            def exponentials(i):
+                row_max = small.tile([P, 1], F32, name="row_max")
+                nc.vector.tensor_reduce(out=row_max[:], in_=part_max[i][:], axis=AXIS.X, op=ALU.max)
+                shift = small.tile([P, 1], F32, name="shift")
+                nc.scalar.mul(shift[:], row_max[:], -SCALE)
                 for part in range(KEY_PARTS):
-                    nc.vector.tensor_reduce(out=part_max[:, part : part + 1], in_=scores[i, part][:], axis=AXIS.X, op=ALU.max)
-                row_max = small.tile([P, 1], F32)
-                nc.vector.tensor_reduce(out=row_max[:], in_=part_max[:], axis=AXIS.X, op=ALU.max)
-                shift = small.tile([P, 1], F32)
-                nc.vector.tensor_scalar(out=shift[:], in0=row_max[:], scalar1=-SCALE, scalar2=None, op0=ALU.mult)
-                part_sum = small.tile([P, KEY_PARTS], F32)
-                for part in range(KEY_PARTS):
+                    weight = const.tile([P, BANK], F32, name="weight%d%d" % (i, part))
                     nc.scalar.activation(
-                        out=weights[:, i, part * BANK : (part + 1) * BANK],
-                        in_=scores[i, part][:],
+                        out=weight[:],
+                        in_=scores[i, part],
                         func=ACT.Exp,
                         bias=shift[:],
                         scale=SCALE,
-                        accum_out=part_sum[:, part : part + 1],
+                        accum_out=part_sum[i][:, part : part + 1],
                     )
-                sums[i] = part_sum
+                    weights[i, part] = weight
 
-            for i in range(2):
-                row_sum = small.tile([P, 1], F32)
-                nc.vector.tensor_reduce(out=row_sum[:], in_=sums[i][:], axis=AXIS.X, op=ALU.add)
-                inverse = small.tile([P, 1], F32)
+            out_rows = out.rearrange("(p i) j -> p i j", i=2)
+
+            def store(i):
+                row_sum = small.tile([P, 1], F32, name="row_sum")
+                nc.vector.tensor_reduce(out=row_sum[:], in_=part_sum[i][:], axis=AXIS.X, op=ALU.add)
+                inverse = small.tile([P, 1], F32, name="inverse")
                 nc.vector.reciprocal(out=inverse[:], in_=row_sum[:])
                 for part in range(KEY_PARTS):
                     cols = slice(part * BANK, (part + 1) * BANK)
                     nc.vector.scalar_tensor_tensor(
-                        out=weights[:, i, cols],
-                        in0=weights[:, i, cols],
+                        out=weights[i, part][:],
+                        in0=weights[i, part][:],
                         scalar=inverse[:],
                         in1=prior_all[:, cols],
                         op0=ALU.mult,
                         op1=ALU.mult,
                     )
-                    nc.sync.dma_start(out=out_rows[:, i, cols], in_=weights[:, i, cols])
+                    nc.sync.dma_start(out=out_rows[:, i, cols], in_=weights[i, part][:])
+
+            score(0, 0)
+            score(1, 0)
+            quantise_keys(1)
+            maximum(0, 0)
+            score(0, 1)
+            score(1, 1)
+            quantise_keys(2)
+            maximum(0, 1)
+            score(0, 2)
+            score(1, 2)
+            maximum(0, 2)
+            exponentials(0)
+            for part in range(KEY_PARTS):
+                maximum(1, part)
+            exponentials(1)
+            store(0)
+            store(1)

@@ -25,11 +25,12 @@ SCALE = WIDTH ** -0.5
 CHUNKS = (1, 1, 2) + 6 * (4,) + (2, 1, 1)
 LONG = max(CHUNKS)
 RAW_BUFS = {1: 6, 2: 3, 4: 9}
-PERM_BUFS = 4
+PERM_BUFS = 7
 STAGE_BUFS = 10
-PACKED_BUFS = 9
+PACKED_BUFS = 10
 RING = 6
 KEY_PARTS = KEYS // BANK
+END_STEPS = 4
 STEP = 3
 
 X_WORDS = PAIR
@@ -139,10 +140,12 @@ def tile_visualdeconfounder_pa_k_kernel(tc, x, Wy_w, Wy_b, k, prior, out):
             banks = {}
             staged = {}
             packed = {}
+            quantised = set()
             key_staged = {}
             key_packed = {}
 
             def quantise(b, p):
+                quantised.add((b, p))
                 if p not in packed:
                     codes = packed_pool.tile([P, X_WORDS + W_WORDS], U32, align_bytes=64, name="codes")
                     scales = packed_pool.tile([P, X_WORDS + W_WORDS], U8, align_bytes=64, name="scales")
@@ -185,27 +188,29 @@ def tile_visualdeconfounder_pa_k_kernel(tc, x, Wy_w, Wy_b, k, prior, out):
                 permute(n)
                 permute_in_place(n)
             waiting = list(range(PASSES))
-            quantised = set()
             for s in range(len(steps) + 2):
                 done = [p for p in waiting if all((b, p) in quantised for b in range(len(row_blocks)))]
                 ahead = starts[s + 1] if s + 1 < len(steps) else []
                 for n in ahead:
                     permute(n)
                 if s >= 2:
-                    for n, b, p, g in steps[s - 2]:
+                    for n, b, p, g in steps[s - 2][:1]:
                         quantise(b, p)
-                        quantised.add((b, p))
                 for n in ahead:
                     permute_in_place(n)
-                for p in done[: 1 if s < len(steps) else None]:
-                    multiply_pass(p)
-                    waiting.remove(p)
+                if s >= 2:
+                    for n, b, p, g in steps[s - 2][1:]:
+                        quantise(b, p)
+                if s % 2 == 0 or s >= len(steps) - END_STEPS:
+                    for p in done[: 2 if s < len(steps) else None]:
+                        multiply_pass(p)
+                        waiting.remove(p)
                 if s < len(steps):
                     for n, b, p, g in steps[s]:
                         transpose_atom(n, b, p, g)
                     for n, b, p, g in steps[s]:
                         copy_out(b, p)
-                if s == len(steps):
+                if s == len(steps) - 1:
                     stage_in_keys(0)
             for p in waiting:
                 multiply_pass(p)
@@ -228,16 +233,16 @@ def tile_visualdeconfounder_pa_k_kernel(tc, x, Wy_w, Wy_b, k, prior, out):
             stage_in_keys(1)
             stage_in_keys(2)
             q_packed = []
-            for i in range(2):
+
+            def quantise_q(i):
                 grouped = const.tile([P, P, Q_TILES], BF16, align_bytes=64, name="q_grouped%d" % i)
                 nc.vector.tensor_copy(out=grouped[:], in_=q_planes[i][:].rearrange("p t c -> p c t"))
                 codes = const.tile([P, P], U32, align_bytes=64, name="q_codes%d" % i)
                 scales = const.tile([P, P], U8, align_bytes=64, name="q_scales%d" % i)
-                q_packed.append((codes, scales, grouped))
-            for codes, scales, grouped in q_packed:
                 nc.vector.quantize_mx(
                     out=codes[:].bitcast(FP8X4), scales=scales[:], in_=grouped[:].rearrange("p c t -> p (c t)")
                 )
+                q_packed.append((codes, scales))
 
             scores = {}
 
@@ -299,16 +304,17 @@ def tile_visualdeconfounder_pa_k_kernel(tc, x, Wy_w, Wy_b, k, prior, out):
                     )
                     nc.sync.dma_start(out=out_rows[:, i, cols], in_=weights[i, part][:])
 
+            quantise_q(0)
             score(0, 0)
-            score(1, 0)
             quantise_keys(1)
-            maximum(0, 0)
             score(0, 1)
-            score(1, 1)
+            maximum(0, 0)
             quantise_keys(2)
-            maximum(0, 1)
             score(0, 2)
-            score(1, 2)
+            quantise_q(1)
+            for part in range(KEY_PARTS):
+                score(1, part)
+            maximum(0, 1)
             maximum(0, 2)
             exponentials(0)
             for part in range(KEY_PARTS):

from contextlib import ExitStack

import concourse.mybir as mybir
from concourse.masks import make_identity

F32 = mybir.dt.float32
BF16 = mybir.dt.bfloat16
U32 = mybir.dt.uint32
U8 = mybir.dt.uint8
FP8X4 = mybir.dt.float8_e4m3fn_x4
ACT = mybir.ActivationFunctionType
ALU = mybir.AluOpType
AXIS = mybir.AxisListType

P = 128
PASS = 4 * P
PAIR = 2 * P
BANK = 512

ROWS, FEATURES, WIDTH, KEYS = 256, 16384, 512, 1536
PASSES = FEATURES // PASS
Q_TILES = WIDTH // P
SCALE = WIDTH ** -0.5

CHUNKS = (1, 1, 2) + 6 * (4,) + (2, 1, 1)
LONG = max(CHUNKS)
RAW_BUFS = {1: 6, 2: 3, 4: 9}
PERM_BUFS = 7
STAGE_BUFS = 10
PACKED_BUFS = 10
RING = 6
KEY_PARTS = KEYS // BANK
END_STEPS = 4
STEP = 3

X_WORDS = PAIR
W_WORDS = 2 * PAIR

FLOPS = 2 * ROWS * FEATURES * WIDTH + 2 * ROWS * WIDTH * KEYS


def tile_visualdeconfounder_pa_k_kernel(tc, x, Wy_w, Wy_b, k, prior, out):
    nc = tc.nc
    w_rows = Wy_w.rearrange("(p t) f -> p t f", t=4)
    row_blocks = (x.rearrange("(p i) f -> p i f", i=2), w_rows[:, 0:2, :], w_rows[:, 2:4, :])

    with ExitStack() as ctx:
        ctx.enter_context(tc.manual_schedule())
        const = ctx.enter_context(tc.tile_pool(name="const", bufs=1))
        raw_pool = ctx.enter_context(tc.tile_pool(name="raw", bufs=1))
        perm_pool = ctx.enter_context(tc.tile_pool(name="perm", bufs=4))
        stage = ctx.enter_context(tc.tile_pool(name="stage", bufs=STAGE_BUFS))
        packed_pool = ctx.enter_context(tc.tile_pool(name="packed", bufs=PACKED_BUFS))
        small = ctx.enter_context(tc.tile_pool(name="small", bufs=6))

        def load_unit(first, passes, b):
            raw = raw_pool.tile([P, 2 * passes, PASS], BF16, bufs=RAW_BUFS[passes], name="raw%d" % passes)
            nc.sync.dma_start(
                out=raw[:].rearrange("p (i g) f -> p i (g f)", i=2),
                in_=row_blocks[b][:, :, first * PASS : (first + passes) * PASS],
            )
            return raw

        def load_the_rest():
            nc.sync.dma_start(out=bias_bf16[:], in_=Wy_b.rearrange("(p t) -> p t", t=Q_TILES))
            nc.gpsimd.tensor_copy(out=bias[:], in_=bias_bf16[:])
            for part in range(KEY_PARTS):
                nc.sync.dma_start(
                    out=keys_raw[:, 4 * part : 4 * part + 4, :],
                    in_=k[BANK * part : BANK * (part + 1), :].rearrange("(j p) e -> p j e", p=P),
                )
            nc.sync.dma_start(out=prior_all[:], in_=prior.partition_broadcast(P))

        ident = const.tile([P, P], F32)
        make_identity(nc, ident[:])
        bias_bf16 = const.tile([P, Q_TILES], BF16)
        bias = const.tile([P, Q_TILES], F32)
        warm = const.tile([P, 1], F32)
        nc.vector.memset(warm[:], 0.0)
        nc.scalar.activation(out=warm[:], in_=warm[:], func=ACT.Exp)

        keys_raw = const.tile([P, KEYS // P, WIDTH], BF16)
        prior_all = const.tile([P, KEYS], BF16)
        raws = []
        unit_passes = []
        atoms = []
        for c, passes in enumerate(CHUNKS):
            first = sum(CHUNKS[:c])
            for b in range(len(row_blocks)):
                atoms.extend((len(raws), b, first + g, g) for g in range(passes))
                raws.append(load_unit(first, passes, b))
                unit_passes.append(passes)
        load_the_rest()


        with tc.psum_pool(name="acc", bufs=1) as acc_pool, tc.psum_pool(name="ring", bufs=RING) as ring:
            acc = [acc_pool.tile([P, 2, ROWS], F32, name="acc%d" % u) for u in range(Q_TILES // 2)]

            def transpose_keys(first):
                bank = ring.tile([P, 2, PAIR], F32, name="bank")
                for i in range(2):
                    words = keys_raw[:, first + i, :].bitcast(F32)
                    for u in range(2):
                        nc.tensor.transpose(bank[:, u, i * P : (i + 1) * P], words[:, u : 2 * P : 2], ident[:])
                return bank

            def permute(n):
                seconds = perm_pool.tile([P, 2 * LONG, P], F32, name="seconds")
                words = raws[n][:].bitcast(F32)
                rows = 2 * unit_passes[n]
                nc.vector.tensor_copy(
                    out=seconds[:, 0:rows].rearrange("p r (c h j) -> p r c h j", h=2, j=8),
                    in_=words.rearrange("p r (h c u j) -> p r u c h j", h=2, u=2, j=8)[:, :, 1],
                )
                permuted[n] = (words[:, :, 0:P], seconds[:])

            def permute_in_place(n):
                windows = raws[n][:].bitcast(F32).rearrange("p r (h c u j) -> p r h c u j", h=2, u=2, j=8)
                nc.vector.tensor_copy(out=windows[:, :, 0, :, 1, :], in_=windows[:, :, 1, :, 0, :])

            def transpose_atom(n, b, p, g):
                passes = unit_passes[n]
                bank = ring.tile([P, 2, PAIR], F32, name="bank")
                for i in range(2):
                    for u in range(2):
                        nc.tensor.transpose(
                            bank[:, u, i * P : (i + 1) * P], permuted[n][u][:, i * passes + g, :], ident[:]
                        )
                banks[b, p] = bank

            def copy_out(b, p):
                staged[b, p] = stage.tile([P, 4 * PAIR], BF16, align_bytes=64, name="grouped")
                regroup(nc.scalar.copy, staged[b, p], 0, banks[b, p])

            def regroup(copy, grouped, first_word, bank):
                halves = grouped[:].bitcast(F32)[:, 2 * first_word : 2 * (first_word + PAIR)]
                copy(out=halves.rearrange("p (c u) -> p c u", u=2), in_=bank[:].rearrange("p u c -> p c u"))

            permuted = {}
            banks = {}
            staged = {}
            packed = {}
            quantised = set()
            key_staged = {}
            key_packed = {}

            def quantise(b, p):
                quantised.add((b, p))
                if p not in packed:
                    codes = packed_pool.tile([P, X_WORDS + W_WORDS], U32, align_bytes=64, name="codes")
                    scales = packed_pool.tile([P, X_WORDS + W_WORDS], U8, align_bytes=64, name="scales")
                    packed[p] = (codes, scales)
                cols = slice(b * PAIR, (b + 1) * PAIR)
                nc.vector.quantize_mx(
                    out=packed[p][0][:, cols].bitcast(FP8X4), scales=packed[p][1][:, cols], in_=staged[b, p][:]
                )

            def multiply_pass(g):
                codes, scales = packed[g]
                for t in range(Q_TILES):
                    w_cols = slice(X_WORDS + t * P, X_WORDS + (t + 1) * P)
                    nc.tensor.matmul_mx(
                        out=acc[t // 2][:, t % 2, :],
                        lhsT=codes[:, w_cols].bitcast(FP8X4),
                        lhsT_scale=scales[:, w_cols],
                        rhs=codes[:, 0:X_WORDS].bitcast(FP8X4),
                        rhs_scale=scales[:, 0:X_WORDS],
                        start=(g == 0 and t % 2 == 0),
                        stop=(g == PASSES - 1 and t % 2 == 1),
                    )

            def stage_in_keys(part):
                grouped = const.tile([P, 4 * BANK], BF16, align_bytes=64, name="key_grouped%d" % part)
                for half in range(2):
                    bank = transpose_keys(4 * part + 2 * half)
                    regroup(nc.scalar.copy, grouped, half * PAIR, bank)
                key_staged[part] = grouped

            def quantise_keys(part):
                codes = const.tile([P, BANK], U32, align_bytes=64, name="key_codes%d" % part)
                scales = const.tile([P, BANK], U8, align_bytes=64, name="key_scales%d" % part)
                key_packed[part] = (codes, scales)
                nc.vector.quantize_mx(out=codes[:].bitcast(FP8X4), scales=scales[:], in_=key_staged[part][:])

            steps = [atoms[a : a + STEP] for a in range(0, len(atoms), STEP)]
            starts = [[n for n, b, p, g in step if g == 0] for step in steps]
            for n in starts[0]:
                permute(n)
                permute_in_place(n)
            waiting = list(range(PASSES))
            for s in range(len(steps) + 2):
                done = [p for p in waiting if all((b, p) in quantised for b in range(len(row_blocks)))]
                ahead = starts[s + 1] if s + 1 < len(steps) else []
                for n in ahead:
                    permute(n)
                if s >= 2:
                    for n, b, p, g in steps[s - 2][:1]:
                        quantise(b, p)
                for n in ahead:
                    permute_in_place(n)
                if s >= 2:
                    for n, b, p, g in steps[s - 2][1:]:
                        quantise(b, p)
                if s % 2 == 0 or s >= len(steps) - END_STEPS:
                    for p in done[: 2 if s < len(steps) else None]:
                        multiply_pass(p)
                        waiting.remove(p)
                if s < len(steps):
                    for n, b, p, g in steps[s]:
                        transpose_atom(n, b, p, g)
                    for n, b, p, g in steps[s]:
                        copy_out(b, p)
                if s == len(steps) - 1:
                    stage_in_keys(0)
            for p in waiting:
                multiply_pass(p)
            quantise_keys(0)

            q_planes = []
            for i in range(2):
                planes = const.tile([P, Q_TILES, P], BF16, name="q_planes%d" % i)
                q_planes.append(planes)
                for t in range(Q_TILES):
                    source = acc[t // 2][:, t % 2, i * P : (i + 1) * P]
                    if t // 2 == 0:
                        nc.scalar.activation(
                            out=planes[:, t, :], in_=source, func=ACT.Identity, bias=bias[:, t : t + 1]
                        )
                    else:
                        nc.vector.tensor_scalar(
                            out=planes[:, t, :], in0=source, scalar1=bias[:, t : t + 1], scalar2=None, op0=ALU.add
                        )
            stage_in_keys(1)
            stage_in_keys(2)
            q_packed = []

            def quantise_q(i):
                grouped = const.tile([P, P, Q_TILES], BF16, align_bytes=64, name="q_grouped%d" % i)
                nc.vector.tensor_copy(out=grouped[:], in_=q_planes[i][:].rearrange("p t c -> p c t"))
                codes = const.tile([P, P], U32, align_bytes=64, name="q_codes%d" % i)
                scales = const.tile([P, P], U8, align_bytes=64, name="q_scales%d" % i)
                nc.vector.quantize_mx(
                    out=codes[:].bitcast(FP8X4), scales=scales[:], in_=grouped[:].rearrange("p c t -> p (c t)")
                )
                q_packed.append((codes, scales))

            scores = {}

            def score(i, part):
                bank = ring.tile([P, 2, PAIR], F32, name="bank")
                scores[i, part] = bank[:].rearrange("p u c -> p (u c)")
                nc.tensor.matmul_mx(
                    out=scores[i, part],
                    lhsT=q_packed[i][0][:].bitcast(FP8X4),
                    lhsT_scale=q_packed[i][1][:],
                    rhs=key_packed[part][0][:].bitcast(FP8X4),
                    rhs_scale=key_packed[part][1][:],
                    start=True,
                    stop=True,
                )

            part_max = [small.tile([P, KEY_PARTS], F32, name="part_max%d" % i) for i in range(2)]
            part_sum = [small.tile([P, KEY_PARTS], F32, name="part_sum%d" % i) for i in range(2)]
            weights = {}

            def maximum(i, part):
                nc.vector.tensor_reduce(
                    out=part_max[i][:, part : part + 1], in_=scores[i, part], axis=AXIS.X, op=ALU.max
                )

            def exponentials(i):
                row_max = small.tile([P, 1], F32, name="row_max")
                nc.vector.tensor_reduce(out=row_max[:], in_=part_max[i][:], axis=AXIS.X, op=ALU.max)
                shift = small.tile([P, 1], F32, name="shift")
                nc.scalar.mul(shift[:], row_max[:], -SCALE)
                for part in range(KEY_PARTS):
                    weight = const.tile([P, BANK], F32, name="weight%d%d" % (i, part))
                    nc.scalar.activation(
                        out=weight[:],
                        in_=scores[i, part],
                        func=ACT.Exp,
                        bias=shift[:],
                        scale=SCALE,
                        accum_out=part_sum[i][:, part : part + 1],
                    )
                    weights[i, part] = weight

            out_rows = out.rearrange("(p i) j -> p i j", i=2)

            def store(i):
                row_sum = small.tile([P, 1], F32, name="row_sum")
                nc.vector.tensor_reduce(out=row_sum[:], in_=part_sum[i][:], axis=AXIS.X, op=ALU.add)
                inverse = small.tile([P, 1], F32, name="inverse")
                nc.vector.reciprocal(out=inverse[:], in_=row_sum[:])
                for part in range(KEY_PARTS):
                    cols = slice(part * BANK, (part + 1) * BANK)
                    nc.vector.scalar_tensor_tensor(
                        out=weights[i, part][:],
                        in0=weights[i, part][:],
                        scalar=inverse[:],
                        in1=prior_all[:, cols],
                        op0=ALU.mult,
                        op1=ALU.mult,
                    )
                    nc.sync.dma_start(out=out_rows[:, i, cols], in_=weights[i, part][:])

            quantise_q(0)
            score(0, 0)
            quantise_keys(1)
            score(0, 1)
            maximum(0, 0)
            quantise_keys(2)
            score(0, 2)
            quantise_q(1)
            for part in range(KEY_PARTS):
                score(1, part)
            maximum(0, 1)
            maximum(0, 2)
            exponentials(0)
            for part in range(KEY_PARTS):
                maximum(1, part)
            exponentials(1)
            store(0)
            store(1)
